import numpy as np
import ml_dtypes


def mxq(x, axis, fmt="e4m3"):
    dtype, down = {"e4m3": (ml_dtypes.float8_e4m3fn, 7), "e5m2": (ml_dtypes.float8_e5m2, 14)}[fmt]
    v = np.moveaxis(np.asarray(x, np.float32).astype(ml_dtypes.bfloat16).astype(np.float64), axis, -1)
    blocks = v.reshape(v.shape[:-1] + (-1, 32))
    amax = np.abs(blocks).max(-1, keepdims=True)
    byte = np.maximum(np.where(amax > 0, np.frexp(amax)[1] - 1 + 127, 0) - down, 1)
    scale = np.exp2(byte - 127.0)
    codes = (blocks / scale).astype(np.float32).astype(dtype).astype(np.float64)
    return np.moveaxis((codes * scale).reshape(v.shape), -1, axis)


WIDE = False


def mx_kscale(k):
    if not WIDE:
        return np.ones(k)
    levels = np.array([10, -10, 5, -5, 0])
    a = np.random.permutation(np.resize(levels, k // 512 * 4)).reshape(k // 512, 4)
    idx = np.arange(k)
    return np.exp2(a[idx // 512, idx % 128 // 32])


BF16 = ml_dtypes.bfloat16


def bf(x):
    return np.asarray(x, np.float32).astype(BF16)


def f64(x):
    return np.asarray(x).astype(np.float64)


B, L, LV, H = 128, 32, 64, 512
NUM_ITERATIONS = 3
X = 0.25
V = 0.12 * L
A = 0.6 / (np.sqrt(H) * V)


def setup_inputs():
    s = mx_kscale(H)
    return {"text_feat": bf(np.random.standard_normal((B, L, H)) * X * s),
            "vision_proj": bf(np.random.standard_normal((B, 1, H)) * V),
            "Wt": bf(np.random.standard_normal((H, H)) * A / (X * np.sqrt(H)) / s[None, :]),
            "bt": bf(np.random.standard_normal(H) * 0.5 * A)}


def reference(text_feat, vision_proj, Wt, bt):
    vp = f64(vision_proj)
    text_proj = (mxq(f64(text_feat), 2, "e4m3") @ mxq(f64(Wt), 1, "e4m3").T) + f64(bt)
    agreement = np.sum(text_proj * vp, axis=-1, keepdims=True)
    coupling = np.zeros_like(agreement)
    for _ in range(NUM_ITERATIONS - 1):
        coupling = coupling + agreement
    e = np.exp(coupling - coupling.max(axis=1, keepdims=True))
    routing_weights = e / e.sum(axis=1, keepdims=True)
    weighted_vision = routing_weights * vp
    return text_proj, weighted_vision

@@ -1,0 +1,194 @@
+from contextlib import ExitStack
+
+import concourse.mybir as mybir
+from concourse.masks import make_identity
+
+F32 = mybir.dt.float32
+BF16 = mybir.dt.bfloat16
+U32 = mybir.dt.uint32
+U8 = mybir.dt.uint8
+FP8X4 = mybir.dt.float8_e4m3fn_x4
+ALU = mybir.AluOpType
+ACT = mybir.ActivationFunctionType
+
+P = 128
+L = 32
+H = 512
+GROUP = 4
+N_GROUPS = L // GROUP
+WORDS = H // 2
+
+FLOPS = 2 * P * L * H * H
+
+
+def tile_dynamicroutingfusion_pa_t_kernel(tc, text_feat, vision_proj, Wt, bt, out_0, out_1):
+    nc = tc.nc
+    with ExitStack() as ctx:
+        keep = ctx.enter_context(tc.tile_pool(name="keep", bufs=1))
+        stage = ctx.enter_context(tc.tile_pool(name="stage", bufs=3))
+        psum_t = ctx.enter_context(tc.psum_pool(name="psum_t", bufs=2))
+        psum_acc = ctx.enter_context(tc.psum_pool(name="psum_acc", bufs=6))
+
+        ident = keep.tile([P, P], F32)
+        w_rows = keep.tile([P, GROUP * H], BF16)
+        w_codes = keep.tile([P, H], U32, align_bytes=64)
+        w_scales = keep.tile([P, H], U8, align_bytes=64)
+        text_rows = keep.tile([P, L * H], BF16)
+        x_codes = keep.tile([P, L * P], U32, align_bytes=64)
+        x_scales = keep.tile([P, L * P], U8, align_bytes=64)
+        vp_bf = keep.tile([P, H], BF16)
+        vp = keep.tile([P, H], F32)
+        bias_bf = keep.tile([P, H], BF16)
+        bias = keep.tile([P, H], F32)
+        text_proj = keep.tile([P, L, H], F32)
+        weighted = keep.tile([P, L, H], F32)
+        coupling = keep.tile([P, L], F32)
+        neg_max = keep.tile([P, 1], F32)
+        exps = keep.tile([P, L], F32)
+        exp_sum = keep.tile([P, 1], F32)
+        inv_sum = keep.tile([P, 1], F32)
+        routing = keep.tile([P, L], F32)
+        warm = keep.tile([P, 1], F32)
+
+        def load_text(g):
+            cols = slice(g * GROUP * H, (g + 1) * GROUP * H)
+            nc.sync.dma_start(
+                out=text_rows[:, cols],
+                in_=text_feat[:, g * GROUP : (g + 1) * GROUP, :].rearrange("b l h -> b (l h)"),
+            )
+
+        nc.sync.dma_start(
+            out=w_rows[:].rearrange("p (c k) -> p c k", c=GROUP),
+            in_=Wt.rearrange("(c p) k -> p c k", p=P),
+        )
+        load_text(0)
+        nc.sync.dma_start(out=vp_bf[:], in_=vision_proj.rearrange("b o h -> b (o h)"))
+        load_text(1)
+        nc.sync.dma_start(out=bias_bf[:], in_=bt.partition_broadcast(P))
+        for g in range(2, N_GROUPS):
+            load_text(g)
+
+        make_identity(nc, ident[:])
+        nc.vector.memset(warm[:], 0.0)
+        nc.scalar.activation(out=warm[:], in_=warm[:], func=ACT.Exp)
+        nc.vector.tensor_copy(out=vp[:], in_=vp_bf[:])
+        nc.vector.tensor_copy(out=bias[:], in_=bias_bf[:])
+
+        def regroup(rows, first_tile, copy_out):
+            words = rows[:].bitcast(F32)
+            grouped = stage.tile([P, GROUP * H], BF16, align_bytes=64)
+            grouped_words = grouped[:].bitcast(F32)
+            for pair in range(GROUP // 2):
+                bank = psum_t.tile([P, 4 * P], F32)
+                for j in range(2):
+                    for u in range(2):
+                        col = (first_tile + 2 * pair + j) * WORDS + u * P
+                        nc.tensor.transpose(
+                            bank[:, (2 * j + u) * P : (2 * j + u + 1) * P],
+                            words[:, col : col + P],
+                            ident[:],
+                        )
+                copy_out(
+                    out=grouped_words[:, pair * 4 * P : (pair + 1) * 4 * P].rearrange(
+                        "p (j r u) -> p j r u", j=2, u=2
+                    ),
+                    in_=bank[:].rearrange("p (j u r) -> p j r u", j=2, u=2),
+                )
+            return grouped
+
+        def quantise(grouped, codes, scales):
+            nc.vector.quantize_mx(out=codes.bitcast(FP8X4), scales=scales, in_=grouped[:])
+
+        def quantise_text(g, grouped):
+            cols = slice(g * GROUP * P, (g + 1) * GROUP * P)
+            quantise(grouped, x_codes[:, cols], x_scales[:, cols])
+
+        def project(g):
+            sums = []
+            for l in range(g * GROUP, (g + 1) * GROUP):
+                acc = psum_acc.tile([P, H], F32)
+                nc.tensor.matmul_mx(
+                    out=acc[:],
+                    lhsT=x_codes[:, l * P : (l + 1) * P].bitcast(FP8X4),
+                    lhsT_scale=x_scales[:, l * P : (l + 1) * P],
+                    rhs=w_codes[:].bitcast(FP8X4),
+                    rhs_scale=w_scales[:],
+                    start=True,
+                    stop=True,
+                )
+                nc.vector.scalar_tensor_tensor(
+                    out=weighted[:, l, :],
+                    in0=acc[:],
+                    scalar=2.0,
+                    in1=vp[:],
+                    op0=ALU.mult,
+                    op1=ALU.mult,
+                    accum_out=coupling[:, l : l + 1],
+                )
+                sums.append(acc)
+            return sums
+
+        def add_bias_off_vector(g, sums):
+            tiles = slice(g * GROUP, (g + 1) * GROUP)
+            for j in range(GROUP):
+                nc.scalar.copy(out=text_proj[:, g * GROUP + j, :], in_=sums[j][:])
+            nc.gpsimd.tensor_tensor(
+                out=text_proj[:, tiles, :],
+                in0=text_proj[:, tiles, :],
+                in1=bias[:].unsqueeze(1).to_broadcast([P, GROUP, H]),
+                op=ALU.add,
+            )
+            nc.sync.dma_start(out=out_0[:, tiles, :], in_=text_proj[:, tiles, :])
+
+        def add_bias_on_vector(g, sums):
+            tiles = slice(g * GROUP, (g + 1) * GROUP)
+            for j in range(GROUP):
+                nc.vector.tensor_tensor(
+                    out=text_proj[:, g * GROUP + j, :], in0=sums[j][:], in1=bias[:], op=ALU.add
+                )
+            nc.sync.dma_start(out=out_0[:, tiles, :], in_=text_proj[:, tiles, :])
+
+        quantise(regroup(w_rows, 0, nc.vector.tensor_copy), w_codes[:], w_scales[:])
+        grouped_of = {0: regroup(text_rows, 0, nc.scalar.copy)}
+        quantise_text(0, grouped_of[0])
+        grouped_of[1] = regroup(text_rows, GROUP, nc.scalar.copy)
+        last_sums = None
+        for g in range(N_GROUPS):
+            if g + 2 < N_GROUPS:
+                grouped_of[g + 2] = regroup(text_rows, (g + 2) * GROUP, nc.scalar.copy)
+            if g + 1 < N_GROUPS:
+                quantise_text(g + 1, grouped_of[g + 1])
+            sums = project(g)
+            if g + 1 < N_GROUPS:
+                add_bias_off_vector(g, sums)
+            else:
+                last_sums = sums
+
+        nc.vector.tensor_reduce(
+            out=neg_max[:], in_=coupling[:], axis=mybir.AxisListType.X, op=ALU.max, negate=True
+        )
+        nc.scalar.activation(
+            out=exps[:], in_=coupling[:], func=ACT.Exp, bias=neg_max[:], scale=1.0, accum_out=exp_sum[:]
+        )
+        nc.vector.reciprocal(out=inv_sum[:], in_=exp_sum[:])
+        nc.vector.tensor_scalar(
+            out=routing[:], in0=exps[:], scalar1=inv_sum[:, 0:1], scalar2=None, op0=ALU.mult
+        )
+
+        for g in range(N_GROUPS):
+            tiles = slice(g * GROUP, (g + 1) * GROUP)
+            for l in range(g * GROUP, (g + 1) * GROUP):
+                if l % 2 == 0:
+                    nc.scalar.activation(
+                        out=weighted[:, l, :], in_=vp[:], func=ACT.Copy, scale=routing[:, l : l + 1]
+                    )
+                else:
+                    nc.vector.tensor_scalar(
+                        out=weighted[:, l, :],
+                        in0=vp[:],
+                        scalar1=routing[:, l : l + 1],
+                        scalar2=None,
+                        op0=ALU.mult,
+                    )
+            nc.scalar.dma_start(out=out_1[:, tiles, :], in_=weighted[:, tiles, :])
+        add_bias_on_vector(N_GROUPS - 1, last_sums)

@@ -17,6 +17,7 @@ H = 512
 GROUP = 4
 N_GROUPS = L // GROUP
 WORDS = H // 2
+GPSIMD_SHARE = 2
 
 FLOPS = 2 * P * L * H * H
 
@@ -28,8 +29,12 @@ def tile_dynamicroutingfusion_pa_t_kernel(tc, text_feat, vision_proj, Wt, bt, ou
         stage = ctx.enter_context(tc.tile_pool(name="stage", bufs=3))
         psum_t = ctx.enter_context(tc.psum_pool(name="psum_t", bufs=2))
         psum_acc = ctx.enter_context(tc.psum_pool(name="psum_acc", bufs=6))
+        ctx.enter_context(tc.manual_schedule())
 
         ident = keep.tile([P, P], F32)
+        ones = keep.tile([P, P], BF16)
+        bt_rows = keep.tile([P, H], BF16)
+        bias = keep.tile([P, H], F32)
         w_rows = keep.tile([P, GROUP * H], BF16)
         w_codes = keep.tile([P, H], U32, align_bytes=64)
         w_scales = keep.tile([P, H], U8, align_bytes=64)
@@ -38,8 +43,6 @@ def tile_dynamicroutingfusion_pa_t_kernel(tc, text_feat, vision_proj, Wt, bt, ou
         x_scales = keep.tile([P, L * P], U8, align_bytes=64)
         vp_bf = keep.tile([P, H], BF16)
         vp = keep.tile([P, H], F32)
-        bias_bf = keep.tile([P, H], BF16)
-        bias = keep.tile([P, H], F32)
         text_proj = keep.tile([P, L, H], F32)
         weighted = keep.tile([P, L, H], F32)
         coupling = keep.tile([P, L], F32)
@@ -63,16 +66,18 @@ def tile_dynamicroutingfusion_pa_t_kernel(tc, text_feat, vision_proj, Wt, bt, ou
         )
         load_text(0)
         nc.sync.dma_start(out=vp_bf[:], in_=vision_proj.rearrange("b o h -> b (o h)"))
-        load_text(1)
-        nc.sync.dma_start(out=bias_bf[:], in_=bt.partition_broadcast(P))
-        for g in range(2, N_GROUPS):
+        for g in range(1, N_GROUPS):
             load_text(g)
 
         make_identity(nc, ident[:])
+        nc.vector.memset(bt_rows[:], 0.0)
+        nc.scalar.dma_start(out=bt_rows[0:1, :], in_=bt.rearrange("(o h) -> o h", o=1))
+        nc.vector.memset(ones[:], 1.0)
         nc.vector.memset(warm[:], 0.0)
         nc.scalar.activation(out=warm[:], in_=warm[:], func=ACT.Exp)
-        nc.vector.tensor_copy(out=vp[:], in_=vp_bf[:])
-        nc.vector.tensor_copy(out=bias[:], in_=bias_bf[:])
+        acc = psum_acc.tile([P, H], F32)
+        nc.tensor.matmul(out=acc[:], lhsT=ones[:], rhs=bt_rows[:], start=True, stop=True)
+        nc.scalar.copy(out=bias[:], in_=acc[:])
 
         def regroup(rows, first_tile, copy_out):
             words = rows[:].bitcast(F32)
@@ -104,8 +109,8 @@ def tile_dynamicroutingfusion_pa_t_kernel(tc, text_feat, vision_proj, Wt, bt, ou
             quantise(grouped, x_codes[:, cols], x_scales[:, cols])
 
         def project(g):
-            sums = []
-            for l in range(g * GROUP, (g + 1) * GROUP):
+            for j in range(GROUP):
+                l = g * GROUP + j
                 acc = psum_acc.tile([P, H], F32)
                 nc.tensor.matmul_mx(
                     out=acc[:],
@@ -125,44 +130,29 @@ def tile_dynamicroutingfusion_pa_t_kernel(tc, text_feat, vision_proj, Wt, bt, ou
                     op1=ALU.mult,
                     accum_out=coupling[:, l : l + 1],
                 )
-                sums.append(acc)
-            return sums
-
-        def add_bias_off_vector(g, sums):
+                if j < GPSIMD_SHARE:
+                    nc.scalar.copy(out=text_proj[:, l, :], in_=acc[:])
+                    nc.gpsimd.tensor_tensor(
+                        out=text_proj[:, l, :], in0=text_proj[:, l, :], in1=bias[:], op=ALU.add
+                    )
+                else:
+                    nc.vector.tensor_tensor(
+                        out=text_proj[:, l, :], in0=acc[:], in1=bias[:], op=ALU.add
+                    )
             tiles = slice(g * GROUP, (g + 1) * GROUP)
-            for j in range(GROUP):
-                nc.scalar.copy(out=text_proj[:, g * GROUP + j, :], in_=sums[j][:])
-            nc.gpsimd.tensor_tensor(
-                out=text_proj[:, tiles, :],
-                in0=text_proj[:, tiles, :],
-                in1=bias[:].unsqueeze(1).to_broadcast([P, GROUP, H]),
-                op=ALU.add,
-            )
-            nc.sync.dma_start(out=out_0[:, tiles, :], in_=text_proj[:, tiles, :])
-
-        def add_bias_on_vector(g, sums):
-            tiles = slice(g * GROUP, (g + 1) * GROUP)
-            for j in range(GROUP):
-                nc.vector.tensor_tensor(
-                    out=text_proj[:, g * GROUP + j, :], in0=sums[j][:], in1=bias[:], op=ALU.add
-                )
             nc.sync.dma_start(out=out_0[:, tiles, :], in_=text_proj[:, tiles, :])
 
         quantise(regroup(w_rows, 0, nc.vector.tensor_copy), w_codes[:], w_scales[:])
         grouped_of = {0: regroup(text_rows, 0, nc.scalar.copy)}
         quantise_text(0, grouped_of[0])
+        nc.vector.tensor_copy(out=vp[:], in_=vp_bf[:])
         grouped_of[1] = regroup(text_rows, GROUP, nc.scalar.copy)
-        last_sums = None
         for g in range(N_GROUPS):
             if g + 2 < N_GROUPS:
                 grouped_of[g + 2] = regroup(text_rows, (g + 2) * GROUP, nc.scalar.copy)
             if g + 1 < N_GROUPS:
                 quantise_text(g + 1, grouped_of[g + 1])
-            sums = project(g)
-            if g + 1 < N_GROUPS:
-                add_bias_off_vector(g, sums)
-            else:
-                last_sums = sums
+            project(g)
 
         nc.vector.tensor_reduce(
             out=neg_max[:], in_=coupling[:], axis=mybir.AxisListType.X, op=ALU.max, negate=True
@@ -176,7 +166,6 @@ def tile_dynamicroutingfusion_pa_t_kernel(tc, text_feat, vision_proj, Wt, bt, ou
         )
 
         for g in range(N_GROUPS):
-            tiles = slice(g * GROUP, (g + 1) * GROUP)
             for l in range(g * GROUP, (g + 1) * GROUP):
                 if l % 2 == 0:
                     nc.scalar.activation(
@@ -190,5 +179,5 @@ def tile_dynamicroutingfusion_pa_t_kernel(tc, text_feat, vision_proj, Wt, bt, ou
                         scalar2=None,
                         op0=ALU.mult,
                     )
-            nc.scalar.dma_start(out=out_1[:, tiles, :], in_=weighted[:, tiles, :])
-        add_bias_on_vector(N_GROUPS - 1, last_sums)
+            tiles = slice(g * GROUP, (g + 1) * GROUP)
+            nc.sync.dma_start(out=out_1[:, tiles, :], in_=weighted[:, tiles, :])

@@ -60,6 +60,8 @@ def tile_dynamicroutingfusion_pa_t_kernel(tc, text_feat, vision_proj, Wt, bt, ou
                 in_=text_feat[:, g * GROUP : (g + 1) * GROUP, :].rearrange("b l h -> b (l h)"),
             )
 
+        nc.vector.memset(bt_rows[:], 0.0)
+        nc.sync.dma_start(out=bt_rows[0:1, :], in_=bt.rearrange("(o h) -> o h", o=1))
         nc.sync.dma_start(
             out=w_rows[:].rearrange("p (c k) -> p c k", c=GROUP),
             in_=Wt.rearrange("(c p) k -> p c k", p=P),
@@ -70,8 +72,6 @@ def tile_dynamicroutingfusion_pa_t_kernel(tc, text_feat, vision_proj, Wt, bt, ou
             load_text(g)
 
         make_identity(nc, ident[:])
-        nc.vector.memset(bt_rows[:], 0.0)
-        nc.scalar.dma_start(out=bt_rows[0:1, :], in_=bt.rearrange("(o h) -> o h", o=1))
         nc.vector.memset(ones[:], 1.0)
         nc.vector.memset(warm[:], 0.0)
         nc.scalar.activation(out=warm[:], in_=warm[:], func=ACT.Exp)
@@ -108,7 +108,15 @@ def tile_dynamicroutingfusion_pa_t_kernel(tc, text_feat, vision_proj, Wt, bt, ou
             cols = slice(g * GROUP * P, (g + 1) * GROUP * P)
             quantise(grouped, x_codes[:, cols], x_scales[:, cols])
 
-        def project(g):
+        def add_bias_on_vector(l, acc):
+            nc.vector.tensor_tensor(out=text_proj[:, l, :], in0=acc[:], in1=bias[:], op=ALU.add)
+
+        def store_text_proj(g):
+            tiles = slice(g * GROUP, (g + 1) * GROUP)
+            nc.sync.dma_start(out=out_0[:, tiles, :], in_=text_proj[:, tiles, :])
+
+        def project(g, vector_adds_later):
+            waiting = []
             for j in range(GROUP):
                 l = g * GROUP + j
                 acc = psum_acc.tile([P, H], F32)
@@ -135,24 +143,25 @@ def tile_dynamicroutingfusion_pa_t_kernel(tc, text_feat, vision_proj, Wt, bt, ou
                     nc.gpsimd.tensor_tensor(
                         out=text_proj[:, l, :], in0=text_proj[:, l, :], in1=bias[:], op=ALU.add
                     )
+                elif vector_adds_later:
+                    waiting.append((l, acc))
                 else:
-                    nc.vector.tensor_tensor(
-                        out=text_proj[:, l, :], in0=acc[:], in1=bias[:], op=ALU.add
-                    )
-            tiles = slice(g * GROUP, (g + 1) * GROUP)
-            nc.sync.dma_start(out=out_0[:, tiles, :], in_=text_proj[:, tiles, :])
+                    add_bias_on_vector(l, acc)
+            return waiting
 
         quantise(regroup(w_rows, 0, nc.vector.tensor_copy), w_codes[:], w_scales[:])
         grouped_of = {0: regroup(text_rows, 0, nc.scalar.copy)}
         quantise_text(0, grouped_of[0])
-        nc.vector.tensor_copy(out=vp[:], in_=vp_bf[:])
+        nc.scalar.copy(out=vp[:], in_=vp_bf[:])
         grouped_of[1] = regroup(text_rows, GROUP, nc.scalar.copy)
         for g in range(N_GROUPS):
             if g + 2 < N_GROUPS:
                 grouped_of[g + 2] = regroup(text_rows, (g + 2) * GROUP, nc.scalar.copy)
             if g + 1 < N_GROUPS:
                 quantise_text(g + 1, grouped_of[g + 1])
-            project(g)
+            waiting = project(g, vector_adds_later=(g == N_GROUPS - 1))
+            if not waiting:
+                store_text_proj(g)
 
         nc.vector.tensor_reduce(
             out=neg_max[:], in_=coupling[:], axis=mybir.AxisListType.X, op=ALU.max, negate=True
@@ -160,6 +169,9 @@ def tile_dynamicroutingfusion_pa_t_kernel(tc, text_feat, vision_proj, Wt, bt, ou
         nc.scalar.activation(
             out=exps[:], in_=coupling[:], func=ACT.Exp, bias=neg_max[:], scale=1.0, accum_out=exp_sum[:]
         )
+        for l, acc in waiting:
+            add_bias_on_vector(l, acc)
+        store_text_proj(N_GROUPS - 1)
         nc.vector.reciprocal(out=inv_sum[:], in_=exp_sum[:])
         nc.vector.tensor_scalar(
             out=routing[:], in0=exps[:], scalar1=inv_sum[:, 0:1], scalar2=None, op0=ALU.mult

@@ -115,52 +115,55 @@ def tile_dynamicroutingfusion_pa_t_kernel(tc, text_feat, vision_proj, Wt, bt, ou
             tiles = slice(g * GROUP, (g + 1) * GROUP)
             nc.sync.dma_start(out=out_0[:, tiles, :], in_=text_proj[:, tiles, :])
 
-        def project(g, vector_adds_later):
-            waiting = []
-            for j in range(GROUP):
-                l = g * GROUP + j
-                acc = psum_acc.tile([P, H], F32)
-                nc.tensor.matmul_mx(
-                    out=acc[:],
-                    lhsT=x_codes[:, l * P : (l + 1) * P].bitcast(FP8X4),
-                    lhsT_scale=x_scales[:, l * P : (l + 1) * P],
-                    rhs=w_codes[:].bitcast(FP8X4),
-                    rhs_scale=w_scales[:],
-                    start=True,
-                    stop=True,
-                )
-                nc.vector.scalar_tensor_tensor(
-                    out=weighted[:, l, :],
-                    in0=acc[:],
-                    scalar=2.0,
-                    in1=vp[:],
-                    op0=ALU.mult,
-                    op1=ALU.mult,
-                    accum_out=coupling[:, l : l + 1],
-                )
-                if j < GPSIMD_SHARE:
-                    nc.scalar.copy(out=text_proj[:, l, :], in_=acc[:])
-                    nc.gpsimd.tensor_tensor(
-                        out=text_proj[:, l, :], in0=text_proj[:, l, :], in1=bias[:], op=ALU.add
-                    )
-                elif vector_adds_later:
-                    waiting.append((l, acc))
-                else:
-                    add_bias_on_vector(l, acc)
-            return waiting
+        def multiply_and_sum(l):
+            acc = psum_acc.tile([P, H], F32)
+            nc.tensor.matmul_mx(
+                out=acc[:],
+                lhsT=x_codes[:, l * P : (l + 1) * P].bitcast(FP8X4),
+                lhsT_scale=x_scales[:, l * P : (l + 1) * P],
+                rhs=w_codes[:].bitcast(FP8X4),
+                rhs_scale=w_scales[:],
+                start=True,
+                stop=True,
+            )
+            nc.vector.scalar_tensor_tensor(
+                out=weighted[:, l, :],
+                in0=acc[:],
+                scalar=2.0,
+                in1=vp[:],
+                op0=ALU.mult,
+                op1=ALU.mult,
+                accum_out=coupling[:, l : l + 1],
+            )
+            return acc
+
+        def add_bias_off_vector(l, acc):
+            nc.scalar.copy(out=text_proj[:, l, :], in_=acc[:])
+            nc.gpsimd.tensor_tensor(
+                out=text_proj[:, l, :], in0=text_proj[:, l, :], in1=bias[:], op=ALU.add
+            )
 
         quantise(regroup(w_rows, 0, nc.vector.tensor_copy), w_codes[:], w_scales[:])
         grouped_of = {0: regroup(text_rows, 0, nc.scalar.copy)}
         quantise_text(0, grouped_of[0])
         nc.scalar.copy(out=vp[:], in_=vp_bf[:])
         grouped_of[1] = regroup(text_rows, GROUP, nc.scalar.copy)
+        waiting = []
         for g in range(N_GROUPS):
             if g + 2 < N_GROUPS:
                 grouped_of[g + 2] = regroup(text_rows, (g + 2) * GROUP, nc.scalar.copy)
-            if g + 1 < N_GROUPS:
-                quantise_text(g + 1, grouped_of[g + 1])
-            waiting = project(g, vector_adds_later=(g == N_GROUPS - 1))
-            if not waiting:
+            for j in range(GROUP):
+                l = g * GROUP + j
+                acc = multiply_and_sum(l)
+                if j == 0 and g + 1 < N_GROUPS:
+                    quantise_text(g + 1, grouped_of[g + 1])
+                if j < GPSIMD_SHARE:
+                    add_bias_off_vector(l, acc)
+                elif g < N_GROUPS - 1:
+                    add_bias_on_vector(l, acc)
+                else:
+                    waiting.append((l, acc))
+            if g < N_GROUPS - 1:
                 store_text_proj(g)
 
         nc.vector.tensor_reduce(

@@ -29,7 +29,6 @@ def tile_dynamicroutingfusion_pa_t_kernel(tc, text_feat, vision_proj, Wt, bt, ou
         stage = ctx.enter_context(tc.tile_pool(name="stage", bufs=3))
         psum_t = ctx.enter_context(tc.psum_pool(name="psum_t", bufs=2))
         psum_acc = ctx.enter_context(tc.psum_pool(name="psum_acc", bufs=6))
-        ctx.enter_context(tc.manual_schedule())
 
         ident = keep.tile([P, P], F32)
         ones = keep.tile([P, P], BF16)

@@ -14,9 +14,10 @@ ACT = mybir.ActivationFunctionType
 P = 128
 L = 32
 H = 512
+WORDS = H // 2
+PAIR = 2
 GROUP = 4
 N_GROUPS = L // GROUP
-WORDS = H // 2
 GPSIMD_SHARE = 2
 
 FLOPS = 2 * P * L * H * H
@@ -29,6 +30,7 @@ def tile_dynamicroutingfusion_pa_t_kernel(tc, text_feat, vision_proj, Wt, bt, ou
         stage = ctx.enter_context(tc.tile_pool(name="stage", bufs=3))
         psum_t = ctx.enter_context(tc.psum_pool(name="psum_t", bufs=2))
         psum_acc = ctx.enter_context(tc.psum_pool(name="psum_acc", bufs=6))
+        ctx.enter_context(tc.manual_schedule())
 
         ident = keep.tile([P, P], F32)
         ones = keep.tile([P, P], BF16)
@@ -52,51 +54,49 @@ def tile_dynamicroutingfusion_pa_t_kernel(tc, text_feat, vision_proj, Wt, bt, ou
         routing = keep.tile([P, L], F32)
         warm = keep.tile([P, 1], F32)
 
-        def load_text(g):
-            cols = slice(g * GROUP * H, (g + 1) * GROUP * H)
+        def load_pair(rows, source, pair):
             nc.sync.dma_start(
-                out=text_rows[:, cols],
-                in_=text_feat[:, g * GROUP : (g + 1) * GROUP, :].rearrange("b l h -> b (l h)"),
+                out=rows[:, pair * PAIR * H : (pair + 1) * PAIR * H].rearrange(
+                    "p (c k) -> p c k", c=PAIR
+                ),
+                in_=source[:, pair * PAIR : (pair + 1) * PAIR, :],
             )
 
+        w_source = Wt.rearrange("(c p) k -> p c k", p=P)
         nc.vector.memset(bt_rows[:], 0.0)
+        load_pair(w_rows, w_source, 0)
         nc.sync.dma_start(out=bt_rows[0:1, :], in_=bt.rearrange("(o h) -> o h", o=1))
-        nc.sync.dma_start(
-            out=w_rows[:].rearrange("p (c k) -> p c k", c=GROUP),
-            in_=Wt.rearrange("(c p) k -> p c k", p=P),
-        )
-        load_text(0)
+        load_pair(w_rows, w_source, 1)
+        load_pair(text_rows, text_feat, 0)
+        load_pair(text_rows, text_feat, 1)
         nc.sync.dma_start(out=vp_bf[:], in_=vision_proj.rearrange("b o h -> b (o h)"))
-        for g in range(1, N_GROUPS):
-            load_text(g)
+        for pair in range(2, L // PAIR):
+            load_pair(text_rows, text_feat, pair)
 
         make_identity(nc, ident[:])
         nc.vector.memset(ones[:], 1.0)
         nc.vector.memset(warm[:], 0.0)
         nc.scalar.activation(out=warm[:], in_=warm[:], func=ACT.Exp)
-        acc = psum_acc.tile([P, H], F32)
-        nc.tensor.matmul(out=acc[:], lhsT=ones[:], rhs=bt_rows[:], start=True, stop=True)
-        nc.scalar.copy(out=bias[:], in_=acc[:])
 
         def regroup(rows, first_tile, copy_out):
             words = rows[:].bitcast(F32)
             grouped = stage.tile([P, GROUP * H], BF16, align_bytes=64)
             grouped_words = grouped[:].bitcast(F32)
-            for pair in range(GROUP // 2):
-                bank = psum_t.tile([P, 4 * P], F32)
-                for j in range(2):
+            for pair in range(GROUP // PAIR):
+                bank = psum_t.tile([P, PAIR * WORDS], F32)
+                for j in range(PAIR):
                     for u in range(2):
-                        col = (first_tile + 2 * pair + j) * WORDS + u * P
+                        col = (first_tile + PAIR * pair + j) * WORDS + u * P
                         nc.tensor.transpose(
                             bank[:, (2 * j + u) * P : (2 * j + u + 1) * P],
                             words[:, col : col + P],
                             ident[:],
                         )
                 copy_out(
-                    out=grouped_words[:, pair * 4 * P : (pair + 1) * 4 * P].rearrange(
-                        "p (j r u) -> p j r u", j=2, u=2
+                    out=grouped_words[:, pair * PAIR * WORDS : (pair + 1) * PAIR * WORDS].rearrange(
+                        "p (j r u) -> p j r u", j=PAIR, u=2
                     ),
-                    in_=bank[:].rearrange("p (j u r) -> p j r u", j=2, u=2),
+                    in_=bank[:].rearrange("p (j u r) -> p j r u", j=PAIR, u=2),
                 )
             return grouped
 
@@ -106,13 +106,6 @@ def tile_dynamicroutingfusion_pa_t_kernel(tc, text_feat, vision_proj, Wt, bt, ou
         def quantise_text(g, grouped):
             cols = slice(g * GROUP * P, (g + 1) * GROUP * P)
             quantise(grouped, x_codes[:, cols], x_scales[:, cols])
-
-        def add_bias_on_vector(l, acc):
-            nc.vector.tensor_tensor(out=text_proj[:, l, :], in0=acc[:], in1=bias[:], op=ALU.add)
-
-        def store_text_proj(g):
-            tiles = slice(g * GROUP, (g + 1) * GROUP)
-            nc.sync.dma_start(out=out_0[:, tiles, :], in_=text_proj[:, tiles, :])
 
         def multiply_and_sum(l):
             acc = psum_acc.tile([P, H], F32)
@@ -142,15 +135,23 @@ def tile_dynamicroutingfusion_pa_t_kernel(tc, text_feat, vision_proj, Wt, bt, ou
                 out=text_proj[:, l, :], in0=text_proj[:, l, :], in1=bias[:], op=ALU.add
             )
 
+        def add_bias_on_vector(l, acc):
+            nc.vector.tensor_tensor(out=text_proj[:, l, :], in0=acc[:], in1=bias[:], op=ALU.add)
+
+        def store_text_proj(g):
+            tiles = slice(g * GROUP, (g + 1) * GROUP)
+            nc.sync.dma_start(out=out_0[:, tiles, :], in_=text_proj[:, tiles, :])
+
         quantise(regroup(w_rows, 0, nc.vector.tensor_copy), w_codes[:], w_scales[:])
         grouped_of = {0: regroup(text_rows, 0, nc.scalar.copy)}
         quantise_text(0, grouped_of[0])
+        spread = psum_acc.tile([P, H], F32, tag="acc")
+        nc.tensor.matmul(out=spread[:], lhsT=ones[:], rhs=bt_rows[:], start=True, stop=True)
+        nc.scalar.copy(out=bias[:], in_=spread[:])
         nc.scalar.copy(out=vp[:], in_=vp_bf[:])
         grouped_of[1] = regroup(text_rows, GROUP, nc.scalar.copy)
         waiting = []
         for g in range(N_GROUPS):
-            if g + 2 < N_GROUPS:
-                grouped_of[g + 2] = regroup(text_rows, (g + 2) * GROUP, nc.scalar.copy)
             for j in range(GROUP):
                 l = g * GROUP + j
                 acc = multiply_and_sum(l)
@@ -164,6 +165,8 @@ def tile_dynamicroutingfusion_pa_t_kernel(tc, text_feat, vision_proj, Wt, bt, ou
                     waiting.append((l, acc))
             if g < N_GROUPS - 1:
                 store_text_proj(g)
+            if g + 2 < N_GROUPS:
+                grouped_of[g + 2] = regroup(text_rows, (g + 2) * GROUP, nc.scalar.copy)
 
         nc.vector.tensor_reduce(
             out=neg_max[:], in_=coupling[:], axis=mybir.AxisListType.X, op=ALU.max, negate=True

from contextlib import ExitStack

import concourse.mybir as mybir
from concourse.masks import make_identity

F32 = mybir.dt.float32
BF16 = mybir.dt.bfloat16
U32 = mybir.dt.uint32
U8 = mybir.dt.uint8
FP8X4 = mybir.dt.float8_e4m3fn_x4
ALU = mybir.AluOpType
ACT = mybir.ActivationFunctionType

P = 128
L = 32
H = 512
WORDS = H // 2
PAIR = 2
GROUP = 4
N_GROUPS = L // GROUP
GPSIMD_SHARE = 2

FLOPS = 2 * P * L * H * H


def tile_dynamicroutingfusion_pa_t_kernel(tc, text_feat, vision_proj, Wt, bt, out_0, out_1):
    nc = tc.nc
    with ExitStack() as ctx:
        keep = ctx.enter_context(tc.tile_pool(name="keep", bufs=1))
        stage = ctx.enter_context(tc.tile_pool(name="stage", bufs=3))
        psum_t = ctx.enter_context(tc.psum_pool(name="psum_t", bufs=2))
        psum_acc = ctx.enter_context(tc.psum_pool(name="psum_acc", bufs=6))
        ctx.enter_context(tc.manual_schedule())

        ident = keep.tile([P, P], F32)
        ones = keep.tile([P, P], BF16)
        bt_rows = keep.tile([P, H], BF16)
        bias = keep.tile([P, H], F32)
        w_rows = keep.tile([P, GROUP * H], BF16)
        w_codes = keep.tile([P, H], U32, align_bytes=64)
        w_scales = keep.tile([P, H], U8, align_bytes=64)
        text_rows = keep.tile([P, L * H], BF16)
        x_codes = keep.tile([P, L * P], U32, align_bytes=64)
        x_scales = keep.tile([P, L * P], U8, align_bytes=64)
        vp_bf = keep.tile([P, H], BF16)
        vp = keep.tile([P, H], F32)
        text_proj = keep.tile([P, L, H], F32)
        weighted = keep.tile([P, L, H], F32)
        coupling = keep.tile([P, L], F32)
        neg_max = keep.tile([P, 1], F32)
        exps = keep.tile([P, L], F32)
        exp_sum = keep.tile([P, 1], F32)
        inv_sum = keep.tile([P, 1], F32)
        routing = keep.tile([P, L], F32)
        warm = keep.tile([P, 1], F32)

        def load_pair(rows, source, pair):
            nc.sync.dma_start(
                out=rows[:, pair * PAIR * H : (pair + 1) * PAIR * H].rearrange(
                    "p (c k) -> p c k", c=PAIR
                ),
                in_=source[:, pair * PAIR : (pair + 1) * PAIR, :],
            )

        w_source = Wt.rearrange("(c p) k -> p c k", p=P)
        nc.vector.memset(bt_rows[:], 0.0)
        load_pair(w_rows, w_source, 0)
        nc.sync.dma_start(out=bt_rows[0:1, :], in_=bt.rearrange("(o h) -> o h", o=1))
        load_pair(w_rows, w_source, 1)
        load_pair(text_rows, text_feat, 0)
        load_pair(text_rows, text_feat, 1)
        nc.sync.dma_start(out=vp_bf[:], in_=vision_proj.rearrange("b o h -> b (o h)"))
        for pair in range(2, L // PAIR):
            load_pair(text_rows, text_feat, pair)

        make_identity(nc, ident[:])
        nc.vector.memset(ones[:], 1.0)
        nc.vector.memset(warm[:], 0.0)
        nc.scalar.activation(out=warm[:], in_=warm[:], func=ACT.Exp)

        def regroup(rows, first_tile, copy_out):
            words = rows[:].bitcast(F32)
            grouped = stage.tile([P, GROUP * H], BF16, align_bytes=64)
            grouped_words = grouped[:].bitcast(F32)
            for pair in range(GROUP // PAIR):
                bank = psum_t.tile([P, PAIR * WORDS], F32)
                for j in range(PAIR):
                    for u in range(2):
                        col = (first_tile + PAIR * pair + j) * WORDS + u * P
                        nc.tensor.transpose(
                            bank[:, (2 * j + u) * P : (2 * j + u + 1) * P],
                            words[:, col : col + P],
                            ident[:],
                        )
                copy_out(
                    out=grouped_words[:, pair * PAIR * WORDS : (pair + 1) * PAIR * WORDS].rearrange(
                        "p (j r u) -> p j r u", j=PAIR, u=2
                    ),
                    in_=bank[:].rearrange("p (j u r) -> p j r u", j=PAIR, u=2),
                )
            return grouped

        def quantise(grouped, codes, scales):
            nc.vector.quantize_mx(out=codes.bitcast(FP8X4), scales=scales, in_=grouped[:])

        def quantise_text(g, grouped):
            cols = slice(g * GROUP * P, (g + 1) * GROUP * P)
            quantise(grouped, x_codes[:, cols], x_scales[:, cols])

        def multiply_and_sum(l):
            acc = psum_acc.tile([P, H], F32)
            nc.tensor.matmul_mx(
                out=acc[:],
                lhsT=x_codes[:, l * P : (l + 1) * P].bitcast(FP8X4),
                lhsT_scale=x_scales[:, l * P : (l + 1) * P],
                rhs=w_codes[:].bitcast(FP8X4),
                rhs_scale=w_scales[:],
                start=True,
                stop=True,
            )
            nc.vector.scalar_tensor_tensor(
                out=weighted[:, l, :],
                in0=acc[:],
                scalar=2.0,
                in1=vp[:],
                op0=ALU.mult,
                op1=ALU.mult,
                accum_out=coupling[:, l : l + 1],
            )
            return acc

        def add_bias_off_vector(l, acc):
            nc.scalar.copy(out=text_proj[:, l, :], in_=acc[:])
            nc.gpsimd.tensor_tensor(
                out=text_proj[:, l, :], in0=text_proj[:, l, :], in1=bias[:], op=ALU.add
            )

        def add_bias_on_vector(l, acc):
            nc.vector.tensor_tensor(out=text_proj[:, l, :], in0=acc[:], in1=bias[:], op=ALU.add)

        def store_text_proj(g):
            tiles = slice(g * GROUP, (g + 1) * GROUP)
            nc.sync.dma_start(out=out_0[:, tiles, :], in_=text_proj[:, tiles, :])

        quantise(regroup(w_rows, 0, nc.vector.tensor_copy), w_codes[:], w_scales[:])
        grouped_of = {0: regroup(text_rows, 0, nc.scalar.copy)}
        quantise_text(0, grouped_of[0])
        spread = psum_acc.tile([P, H], F32, tag="acc")
        nc.tensor.matmul(out=spread[:], lhsT=ones[:], rhs=bt_rows[:], start=True, stop=True)
        nc.scalar.copy(out=bias[:], in_=spread[:])
        nc.scalar.copy(out=vp[:], in_=vp_bf[:])
        grouped_of[1] = regroup(text_rows, GROUP, nc.scalar.copy)
        waiting = []
        for g in range(N_GROUPS):
            for j in range(GROUP):
                l = g * GROUP + j
                acc = multiply_and_sum(l)
                if j == 0 and g + 1 < N_GROUPS:
                    quantise_text(g + 1, grouped_of[g + 1])
                if j < GPSIMD_SHARE:
                    add_bias_off_vector(l, acc)
                elif g < N_GROUPS - 1:
                    add_bias_on_vector(l, acc)
                else:
                    waiting.append((l, acc))
            if g < N_GROUPS - 1:
                store_text_proj(g)
            if g + 2 < N_GROUPS:
                grouped_of[g + 2] = regroup(text_rows, (g + 2) * GROUP, nc.scalar.copy)

        nc.vector.tensor_reduce(
            out=neg_max[:], in_=coupling[:], axis=mybir.AxisListType.X, op=ALU.max, negate=True
        )
        nc.scalar.activation(
            out=exps[:], in_=coupling[:], func=ACT.Exp, bias=neg_max[:], scale=1.0, accum_out=exp_sum[:]
        )
        for l, acc in waiting:
            add_bias_on_vector(l, acc)
        store_text_proj(N_GROUPS - 1)
        nc.vector.reciprocal(out=inv_sum[:], in_=exp_sum[:])
        nc.vector.tensor_scalar(
            out=routing[:], in0=exps[:], scalar1=inv_sum[:, 0:1], scalar2=None, op0=ALU.mult
        )

        for g in range(N_GROUPS):
            for l in range(g * GROUP, (g + 1) * GROUP):
                if l % 2 == 0:
                    nc.scalar.activation(
                        out=weighted[:, l, :], in_=vp[:], func=ACT.Copy, scale=routing[:, l : l + 1]
                    )
                else:
                    nc.vector.tensor_scalar(
                        out=weighted[:, l, :],
                        in0=vp[:],
                        scalar1=routing[:, l : l + 1],
                        scalar2=None,
                        op0=ALU.mult,
                    )
            tiles = slice(g * GROUP, (g + 1) * GROUP)
            nc.sync.dma_start(out=out_1[:, tiles, :], in_=weighted[:, tiles, :])
